import numpy as np
import ml_dtypes


def mxq(x, axis, fmt="e4m3"):
    dtype, down = {"e4m3": (ml_dtypes.float8_e4m3fn, 7), "e5m2": (ml_dtypes.float8_e5m2, 14)}[fmt]
    v = np.moveaxis(np.asarray(x, np.float32).astype(ml_dtypes.bfloat16).astype(np.float64), axis, -1)
    blocks = v.reshape(v.shape[:-1] + (-1, 32))
    amax = np.abs(blocks).max(-1, keepdims=True)
    byte = np.maximum(np.where(amax > 0, np.frexp(amax)[1] - 1 + 127, 0) - down, 1)
    scale = np.exp2(byte - 127.0)
    codes = (blocks / scale).astype(np.float32).astype(dtype).astype(np.float64)
    return np.moveaxis((codes * scale).reshape(v.shape), -1, axis)


WIDE = False


def mx_kscale(k):
    if not WIDE:
        return np.ones(k)
    levels = np.array([10, -10, 5, -5, 0])
    a = np.random.permutation(np.resize(levels, k // 512 * 4)).reshape(k // 512, 4)
    idx = np.arange(k)
    return np.exp2(a[idx // 512, idx % 128 // 32])


BF16 = ml_dtypes.bfloat16


def bf(x):
    return np.asarray(x, np.float32).astype(BF16)


def f64(x):
    return np.asarray(x).astype(np.float64)


B, IMG, P0, P1, C, F = 2, 256, 8, 16, 2, 512
E0, E1 = IMG // P0, IMG // P1
N0, N1 = E0 * E0, E1 * E1
D0, D1 = P0 * P0 * C, P1 * P1 * C


def setup_inputs():
    s = mx_kscale(D1)
    flat = np.random.standard_normal((B, N1, D1)) * s
    img = flat.reshape(B, E1, E1, P1, P1, C).transpose(0, 1, 3, 2, 4, 5).reshape(B, IMG, IMG, C)
    encoded = img.reshape(B, E0, P0, E0, P0, C).transpose(0, 1, 3, 2, 4, 5).reshape(B, N0, D0)
    return {"encoded": bf(encoded),
            "W": bf(np.random.standard_normal((D1, F)) / np.sqrt(D1) / s[:, None]),
            "b": bf(np.random.standard_normal(F) * 0.3),
            "pos_emb": bf(np.random.standard_normal((N1, F)) * 0.5)}


def reference(encoded, W, b, pos_emb):
    x = f64(encoded).reshape(-1, E0, E0, P0, P0, C)
    img = x.transpose(0, 1, 3, 2, 4, 5).reshape(-1, IMG, IMG, C)
    new_patches = img.reshape(-1, E1, P1, E1, P1, C).transpose(0, 1, 3, 2, 4, 5)
    flat = new_patches.reshape(-1, N1, D1)
    return (mxq(flat, 2, "e4m3") @ mxq(f64(W), 0, "e4m3")) + f64(b) + f64(pos_emb)

@@ -1,0 +1,125 @@
+from contextlib import ExitStack
+
+import concourse.mybir as mybir
+from concourse.masks import make_identity
+
+BF16 = mybir.dt.bfloat16
+F32 = mybir.dt.float32
+U32 = mybir.dt.uint32
+U8 = mybir.dt.uint8
+FP8X4 = mybir.dt.float8_e4m3fn_x4
+ADD = mybir.AluOpType.add
+
+P = 128
+PACK = 4
+IMAGES = 2
+TOKENS = 512
+K = 512
+F = 512
+TOKEN_TILES = TOKENS // P
+CHUNK = 128
+CHUNKS = F // CHUNK
+HALVES = 2
+
+FLOPS = 2 * TOKENS * K * F
+
+
+def tile_resampling_s_kernel(tc, encoded, W, b, pos_emb, out):
+    nc = tc.nc
+    with ExitStack() as ctx:
+        keep = ctx.enter_context(tc.tile_pool(name="keep", bufs=1))
+        psum = ctx.enter_context(tc.psum_pool(name="psum", bufs=1))
+        psum_xt = ctx.enter_context(tc.psum_pool(name="psum_xt", bufs=2))
+
+        ident = keep.tile([P, P], F32)
+        make_identity(nc, ident[:])
+        ones = keep.tile([P, P], BF16)
+        nc.vector.memset(ones[:], 1.0)
+        b_rows = keep.tile([P, F], BF16)
+        nc.vector.memset(b_rows[:], 0.0)
+        nc.scalar.dma_start(out=b_rows[0:1, :], in_=b.unsqueeze(0))
+
+        pair_rows = encoded.rearrange("i (q c) d -> (i q) (c d)", c=2)
+        pair_rows = pair_rows.rearrange("(g p) w -> p g w", p=P)
+        x_raw = []
+        for m in range(TOKEN_TILES):
+            x_raw_m = keep.tile([P, 2, 256], BF16, name="x_raw%d" % m)
+            nc.sync.dma_start(out=x_raw_m[:], in_=pair_rows[:, 2 * m : 2 * m + 2, :])
+            x_raw.append(x_raw_m)
+        pos_sb = keep.tile([P, HALVES, F], BF16)
+        nc.sync.dma_start(out=pos_sb[:], in_=pos_emb.rearrange("(h p) n -> p h n", p=P))
+        w_raw = keep.tile([P, PACK, F], BF16)
+        for u in range(2):
+            nc.sync.dma_start(
+                out=w_raw[:, 2 * u : 2 * u + 2, :],
+                in_=W[256 * u : 256 * u + 256, :].rearrange("(p e) n -> p e n", e=2),
+            )
+
+        bias_ps = psum.tile([P, F], F32)
+        nc.tensor.matmul(out=bias_ps[:], lhsT=ones[:], rhs=b_rows[:], start=True, stop=True)
+
+        x_codes = []
+        x_scales = []
+        for m in range(TOKEN_TILES):
+            x_ord = keep.tile([P, 2, 256], BF16, name="x_ord%d" % m)
+            nc.vector.tensor_copy(
+                out=x_ord[:].rearrange("p g (r c e) -> p g r c e", r=8, c=2),
+                in_=x_raw[m][:].rearrange("p g (c r e) -> p g r c e", c=2, r=8),
+            )
+            xt = psum_xt.tile([P, 2, P], F32)
+            for g in range(2):
+                nc.tensor.transpose(xt[:, g, :], x_ord[:, g, :].bitcast(F32), ident[:])
+            x_grp = keep.tile([P, P * PACK], BF16, name="x_grp%d" % m, align_bytes=64)
+            nc.scalar.copy(
+                out=x_grp[:].bitcast(F32).rearrange("p (a x r) -> p a x r", x=16, r=2),
+                in_=xt[:].rearrange("p g c -> p (g c)").rearrange("p (a r x) -> p a x r", r=2, x=16),
+            )
+            codes = keep.tile([P, P], U32, name="x_codes%d" % m, align_bytes=64)
+            scales = keep.tile([P, P], U8, name="x_scales%d" % m, align_bytes=64)
+            nc.vector.quantize_mx(out=codes[:].bitcast(FP8X4), scales=scales[:], in_=x_grp[:])
+            x_codes.append(codes)
+            x_scales.append(scales)
+
+        posb = keep.tile([P, HALVES, F], F32)
+        nc.vector.tensor_tensor(
+            out=posb[:],
+            in0=bias_ps[:].unsqueeze(1).to_broadcast([P, HALVES, F]),
+            in1=pos_sb[:],
+            op=ADD,
+        )
+
+        out_view = out.rearrange("i (h p) n -> p (i h) n", p=P)
+        for c in range(CHUNKS):
+            cols = slice(c * CHUNK, (c + 1) * CHUNK)
+            w_grp = keep.tile([P, CHUNK, PACK], BF16, name="w_grp%d" % c, align_bytes=64)
+            regroup = nc.vector.tensor_copy if c % 2 == 0 else nc.scalar.copy
+            regroup(
+                out=w_grp[:].rearrange("p (a i) t -> p a t i", i=4),
+                in_=w_raw[:, :, cols].rearrange("p t (a i) -> p a t i", i=4),
+            )
+            w_codes = keep.tile([P, CHUNK], U32, name="w_codes%d" % c, align_bytes=64)
+            w_scales = keep.tile([P, CHUNK], U8, name="w_scales%d" % c, align_bytes=64)
+            nc.vector.quantize_mx(
+                out=w_codes[:].bitcast(FP8X4),
+                scales=w_scales[:],
+                in_=w_grp[:].rearrange("p n t -> p (n t)"),
+            )
+            acc = psum.tile([P, TOKEN_TILES, CHUNK], F32, name="acc%d" % c)
+            for m in range(TOKEN_TILES):
+                nc.tensor.matmul_mx(
+                    out=acc[:, m, :],
+                    lhsT=x_codes[m][:].bitcast(FP8X4),
+                    lhsT_scale=x_scales[m][:],
+                    rhs=w_codes[:].bitcast(FP8X4),
+                    rhs_scale=w_scales[:],
+                    start=True,
+                    stop=True,
+                )
+            res = keep.tile([P, TOKEN_TILES, CHUNK], F32, name="res%d" % c)
+            nc.vector.tensor_tensor(
+                out=res[:].rearrange("p (i h) n -> p i h n", i=IMAGES),
+                in0=acc[:].rearrange("p (i h) n -> p i h n", i=IMAGES),
+                in1=posb[:, :, cols].unsqueeze(1).to_broadcast([P, IMAGES, HALVES, CHUNK]),
+                op=ADD,
+            )
+            nc.sync.dma_start(out=out_view[:, :, cols], in_=res[:])

@@ -17,10 +17,11 @@ TOKENS = 512
 K = 512
 F = 512
 TOKEN_TILES = TOKENS // P
-CHUNK = 128
-CHUNKS = F // CHUNK
-HALVES = 2
+TILES_PER_IMAGE = TOKEN_TILES // IMAGES
 
+W_PARTS = 2
+PART = F // W_PARTS
+VECTOR_COLS = 168
 FLOPS = 2 * TOKENS * K * F
 
 
@@ -29,7 +30,7 @@ def tile_resampling_s_kernel(tc, encoded, W, b, pos_emb, out):
     with ExitStack() as ctx:
         keep = ctx.enter_context(tc.tile_pool(name="keep", bufs=1))
         psum = ctx.enter_context(tc.psum_pool(name="psum", bufs=1))
-        psum_xt = ctx.enter_context(tc.psum_pool(name="psum_xt", bufs=2))
+        ctx.enter_context(tc.manual_schedule())
 
         ident = keep.tile([P, P], F32)
         make_identity(nc, ident[:])
@@ -40,14 +41,14 @@ def tile_resampling_s_kernel(tc, encoded, W, b, pos_emb, out):
         nc.scalar.dma_start(out=b_rows[0:1, :], in_=b.unsqueeze(0))
 
         pair_rows = encoded.rearrange("i (q c) d -> (i q) (c d)", c=2)
-        pair_rows = pair_rows.rearrange("(g p) w -> p g w", p=P)
+        pair_rows = pair_rows.rearrange("(s p h) w -> s p h w", p=P, h=2)
         x_raw = []
-        for m in range(TOKEN_TILES):
-            x_raw_m = keep.tile([P, 2, 256], BF16, name="x_raw%d" % m)
-            nc.sync.dma_start(out=x_raw_m[:], in_=pair_rows[:, 2 * m : 2 * m + 2, :])
-            x_raw.append(x_raw_m)
-        pos_sb = keep.tile([P, HALVES, F], BF16)
-        nc.sync.dma_start(out=pos_sb[:], in_=pos_emb.rearrange("(h p) n -> p h n", p=P))
+        for s in range(TOKEN_TILES):
+            x_raw_s = keep.tile([P, 2, 256], BF16, name="x_raw%d" % s)
+            nc.sync.dma_start(out=x_raw_s[:], in_=pair_rows[s])
+            x_raw.append(x_raw_s)
+        pos_sb = keep.tile([P, TILES_PER_IMAGE, F], BF16)
+        nc.sync.dma_start(out=pos_sb[:], in_=pos_emb.rearrange("(p h) n -> p h n", h=TILES_PER_IMAGE))
         w_raw = keep.tile([P, PACK, F], BF16)
         for u in range(2):
             nc.sync.dma_start(
@@ -55,71 +56,74 @@ def tile_resampling_s_kernel(tc, encoded, W, b, pos_emb, out):
                 in_=W[256 * u : 256 * u + 256, :].rearrange("(p e) n -> p e n", e=2),
             )
 
+        x_grp = []
+        for i in range(IMAGES):
+            xt = psum.tile([P, TILES_PER_IMAGE, 2, P], F32, name="xt%d" % i)
+            for half in range(2):
+                s = 2 * i + half
+                x_ord = keep.tile([P, 2, 256], BF16, name="x_ord%d" % s)
+                nc.vector.tensor_copy(
+                    out=x_ord[:].rearrange("p h (r c e) -> p h r c e", r=8, c=2),
+                    in_=x_raw[s][:].rearrange("p h (c r e) -> p h r c e", c=2, r=8),
+                )
+                for h in range(TILES_PER_IMAGE):
+                    nc.tensor.transpose(xt[:, h, half, :], x_ord[:, h, :].bitcast(F32), ident[:])
+            x_grp_i = keep.tile([P, TILES_PER_IMAGE * P * PACK], BF16, name="x_grp%d" % i, align_bytes=64)
+            nc.scalar.copy(
+                out=x_grp_i[:].bitcast(F32).rearrange("p (a x r) -> p a x r", x=8, r=2),
+                in_=xt[:].rearrange("p h s c -> p (h s c)").rearrange("p (a r x) -> p a x r", r=2, x=8),
+            )
+            x_grp.append(x_grp_i)
+
         bias_ps = psum.tile([P, F], F32)
         nc.tensor.matmul(out=bias_ps[:], lhsT=ones[:], rhs=b_rows[:], start=True, stop=True)
 
         x_codes = []
         x_scales = []
-        for m in range(TOKEN_TILES):
-            x_ord = keep.tile([P, 2, 256], BF16, name="x_ord%d" % m)
-            nc.vector.tensor_copy(
-                out=x_ord[:].rearrange("p g (r c e) -> p g r c e", r=8, c=2),
-                in_=x_raw[m][:].rearrange("p g (c r e) -> p g r c e", c=2, r=8),
-            )
-            xt = psum_xt.tile([P, 2, P], F32)
-            for g in range(2):
-                nc.tensor.transpose(xt[:, g, :], x_ord[:, g, :].bitcast(F32), ident[:])
-            x_grp = keep.tile([P, P * PACK], BF16, name="x_grp%d" % m, align_bytes=64)
-            nc.scalar.copy(
-                out=x_grp[:].bitcast(F32).rearrange("p (a x r) -> p a x r", x=16, r=2),
-                in_=xt[:].rearrange("p g c -> p (g c)").rearrange("p (a r x) -> p a x r", r=2, x=16),
-            )
-            codes = keep.tile([P, P], U32, name="x_codes%d" % m, align_bytes=64)
-            scales = keep.tile([P, P], U8, name="x_scales%d" % m, align_bytes=64)
-            nc.vector.quantize_mx(out=codes[:].bitcast(FP8X4), scales=scales[:], in_=x_grp[:])
+        for i in range(IMAGES):
+            codes = keep.tile([P, TILES_PER_IMAGE * P], U32, name="x_codes%d" % i, align_bytes=64)
+            scales = keep.tile([P, TILES_PER_IMAGE * P], U8, name="x_scales%d" % i, align_bytes=64)
+            nc.vector.quantize_mx(out=codes[:].bitcast(FP8X4), scales=scales[:], in_=x_grp[i][:])
             x_codes.append(codes)
             x_scales.append(scales)
+        posb = keep.tile([P, TILES_PER_IMAGE, F], F32)
+        for h in range(TILES_PER_IMAGE):
+            nc.vector.tensor_tensor(out=posb[:, h, :], in0=bias_ps[:], in1=pos_sb[:, h, :], op=ADD)
 
-        posb = keep.tile([P, HALVES, F], F32)
-        nc.vector.tensor_tensor(
-            out=posb[:],
-            in0=bias_ps[:].unsqueeze(1).to_broadcast([P, HALVES, F]),
-            in1=pos_sb[:],
-            op=ADD,
-        )
-
-        out_view = out.rearrange("i (h p) n -> p (i h) n", p=P)
-        for c in range(CHUNKS):
-            cols = slice(c * CHUNK, (c + 1) * CHUNK)
-            w_grp = keep.tile([P, CHUNK, PACK], BF16, name="w_grp%d" % c, align_bytes=64)
-            regroup = nc.vector.tensor_copy if c % 2 == 0 else nc.scalar.copy
-            regroup(
-                out=w_grp[:].rearrange("p (a i) t -> p a t i", i=4),
-                in_=w_raw[:, :, cols].rearrange("p t (a i) -> p a t i", i=4),
-            )
-            w_codes = keep.tile([P, CHUNK], U32, name="w_codes%d" % c, align_bytes=64)
-            w_scales = keep.tile([P, CHUNK], U8, name="w_scales%d" % c, align_bytes=64)
-            nc.vector.quantize_mx(
-                out=w_codes[:].bitcast(FP8X4),
-                scales=w_scales[:],
-                in_=w_grp[:].rearrange("p n t -> p (n t)"),
-            )
-            acc = psum.tile([P, TOKEN_TILES, CHUNK], F32, name="acc%d" % c)
-            for m in range(TOKEN_TILES):
-                nc.tensor.matmul_mx(
-                    out=acc[:, m, :],
-                    lhsT=x_codes[m][:].bitcast(FP8X4),
-                    lhsT_scale=x_scales[m][:],
-                    rhs=w_codes[:].bitcast(FP8X4),
-                    rhs_scale=w_scales[:],
-                    start=True,
-                    stop=True,
+        w_codes = []
+        w_scales = []
+        for c in range(W_PARTS):
+            w_grp = keep.tile([P, PART, PACK], BF16, name="w_grp%d" % c, align_bytes=64)
+            for copy, lo, hi in ((nc.vector.tensor_copy, 0, VECTOR_COLS), (nc.scalar.copy, VECTOR_COLS, PART)):
+                copy(
+                    out=w_grp[:, lo:hi, :].rearrange("p (a i) t -> p a t i", i=4),
+                    in_=w_raw[:, :, c * PART + lo : c * PART + hi].rearrange("p t (a i) -> p a t i", i=4),
                 )
-            res = keep.tile([P, TOKEN_TILES, CHUNK], F32, name="res%d" % c)
-            nc.vector.tensor_tensor(
-                out=res[:].rearrange("p (i h) n -> p i h n", i=IMAGES),
-                in0=acc[:].rearrange("p (i h) n -> p i h n", i=IMAGES),
-                in1=posb[:, :, cols].unsqueeze(1).to_broadcast([P, IMAGES, HALVES, CHUNK]),
-                op=ADD,
+            codes = keep.tile([P, PART], U32, name="w_codes%d" % c, align_bytes=64)
+            scales = keep.tile([P, PART], U8, name="w_scales%d" % c, align_bytes=64)
+            nc.vector.quantize_mx(
+                out=codes[:].bitcast(FP8X4), scales=scales[:], in_=w_grp[:].rearrange("p n t -> p (n t)")
             )
-            nc.sync.dma_start(out=out_view[:, :, cols], in_=res[:])
+            w_codes.append(codes)
+            w_scales.append(scales)
+
+        for c in range(W_PARTS):
+            cols = slice(c * PART, (c + 1) * PART)
+            for i in range(IMAGES):
+                acc = psum.tile([P, TILES_PER_IMAGE, PART], F32, name="acc%d%d" % (c, i))
+                for h in range(TILES_PER_IMAGE):
+                    tokens = slice(h * P, (h + 1) * P)
+                    nc.tensor.matmul_mx(
+                        out=acc[:, h, :],
+                        lhsT=x_codes[i][:, tokens].bitcast(FP8X4),
+                        lhsT_scale=x_scales[i][:, tokens],
+                        rhs=w_codes[c][:].bitcast(FP8X4),
+                        rhs_scale=w_scales[c][:],
+                        start=True,
+                        stop=True,
+                    )
+                res = keep.tile([P, TILES_PER_IMAGE, PART], F32, name="res%d%d" % (c, i))
+                nc.vector.tensor_tensor(out=res[:], in0=acc[:], in1=posb[:, :, cols], op=ADD)
+                nc.sync.dma_start(
+                    out=out[i].rearrange("(p h) n -> p h n", h=TILES_PER_IMAGE)[:, :, cols], in_=res[:]
+                )

@@ -50,11 +50,10 @@ def tile_resampling_s_kernel(tc, encoded, W, b, pos_emb, out):
         pos_sb = keep.tile([P, TILES_PER_IMAGE, F], BF16)
         nc.sync.dma_start(out=pos_sb[:], in_=pos_emb.rearrange("(p h) n -> p h n", h=TILES_PER_IMAGE))
         w_raw = keep.tile([P, PACK, F], BF16)
-        for u in range(2):
-            nc.sync.dma_start(
-                out=w_raw[:, 2 * u : 2 * u + 2, :],
-                in_=W[256 * u : 256 * u + 256, :].rearrange("(p e) n -> p e n", e=2),
-            )
+        nc.sync.dma_start(
+            out=w_raw[:].rearrange("p (u e) n -> p u (e n)", u=2),
+            in_=W.rearrange("(u p e) n -> p u (e n)", u=2, e=2),
+        )
 
         x_grp = []
         for i in range(IMAGES):

@@ -33,96 +33,108 @@ def tile_resampling_s_kernel(tc, encoded, W, b, pos_emb, out):
         ctx.enter_context(tc.manual_schedule())
 
         ident = keep.tile([P, P], F32)
-        make_identity(nc, ident[:])
         ones = keep.tile([P, P], BF16)
-        nc.vector.memset(ones[:], 1.0)
+        b_row = keep.tile([1, F], BF16)
         b_rows = keep.tile([P, F], BF16)
-        nc.vector.memset(b_rows[:], 0.0)
-        nc.scalar.dma_start(out=b_rows[0:1, :], in_=b.unsqueeze(0))
+        x_raw = [keep.tile([P, 2, 256], BF16, name="x_raw%d" % s) for s in range(TOKEN_TILES)]
+        x_ord = [keep.tile([P, 2, 256], BF16, name="x_ord%d" % s) for s in range(TOKEN_TILES)]
+        xt = [psum.tile([P, TILES_PER_IMAGE, 2, P], F32, name="xt%d" % i) for i in range(IMAGES)]
+        x_cols = TILES_PER_IMAGE * P
+        x_grp = [keep.tile([P, x_cols * PACK], BF16, name="x_grp%d" % i, align_bytes=64) for i in range(IMAGES)]
+        x_codes = [keep.tile([P, x_cols], U32, name="x_codes%d" % i, align_bytes=64) for i in range(IMAGES)]
+        x_scales = [keep.tile([P, x_cols], U8, name="x_scales%d" % i, align_bytes=64) for i in range(IMAGES)]
+        pos_sb = keep.tile([P, TILES_PER_IMAGE, F], BF16)
+        bias_ps = psum.tile([P, F], F32)
+        posb = keep.tile([P, TILES_PER_IMAGE, F], F32)
+        w_raw = keep.tile([P, PACK, F], BF16)
+        w_grp = [keep.tile([P, PART, PACK], BF16, name="w_grp%d" % c, align_bytes=64) for c in range(W_PARTS)]
+        w_codes = [keep.tile([P, PART], U32, name="w_codes%d" % c, align_bytes=64) for c in range(W_PARTS)]
+        w_scales = [keep.tile([P, PART], U8, name="w_scales%d" % c, align_bytes=64) for c in range(W_PARTS)]
 
         pair_rows = encoded.rearrange("i (q c) d -> (i q) (c d)", c=2)
         pair_rows = pair_rows.rearrange("(s p h) w -> s p h w", p=P, h=2)
-        x_raw = []
-        for s in range(TOKEN_TILES):
-            x_raw_s = keep.tile([P, 2, 256], BF16, name="x_raw%d" % s)
-            nc.sync.dma_start(out=x_raw_s[:], in_=pair_rows[s])
-            x_raw.append(x_raw_s)
-        pos_sb = keep.tile([P, TILES_PER_IMAGE, F], BF16)
+
+        def load_x(s):
+            nc.sync.dma_start(out=x_raw[s][:], in_=pair_rows[s])
+
+        def transpose_x(s):
+            nc.vector.tensor_copy(
+                out=x_ord[s][:].rearrange("p h (r c e) -> p h r c e", r=8, c=2),
+                in_=x_raw[s][:].rearrange("p h (c r e) -> p h r c e", c=2, r=8),
+            )
+            for h in range(TILES_PER_IMAGE):
+                nc.tensor.transpose(xt[s // 2][:, h, s % 2, :], x_ord[s][:, h, :].bitcast(F32), ident[:])
+
+        def group_x(i):
+            nc.scalar.copy(
+                out=x_grp[i][:].bitcast(F32).rearrange("p (a x r) -> p a x r", x=8, r=2),
+                in_=xt[i][:].rearrange("p h s c -> p (h s c)").rearrange("p (a r x) -> p a x r", r=2, x=8),
+            )
+
+        def quantise_x(i):
+            nc.vector.quantize_mx(out=x_codes[i][:].bitcast(FP8X4), scales=x_scales[i][:], in_=x_grp[i][:])
+
+        def add_b_to_pos(h):
+            nc.vector.tensor_tensor(out=posb[:, h, :], in0=bias_ps[:], in1=pos_sb[:, h, :], op=ADD)
+
+        def regroup_w(c):
+            for copy, lo, hi in ((nc.vector.tensor_copy, 0, VECTOR_COLS), (nc.scalar.copy, VECTOR_COLS, PART)):
+                copy(
+                    out=w_grp[c][:, lo:hi, :].rearrange("p (a i) t -> p a t i", i=4),
+                    in_=w_raw[:, :, c * PART + lo : c * PART + hi].rearrange("p t (a i) -> p a t i", i=4),
+                )
+
+        def quantise_w(c):
+            nc.vector.quantize_mx(
+                out=w_codes[c][:].bitcast(FP8X4),
+                scales=w_scales[c][:],
+                in_=w_grp[c][:].rearrange("p n t -> p (n t)"),
+            )
+
+        def project(c, i):
+            cols = slice(c * PART, (c + 1) * PART)
+            acc = psum.tile([P, TILES_PER_IMAGE, PART], F32, name="acc%d%d" % (c, i))
+            for h in range(TILES_PER_IMAGE):
+                tokens = slice(h * P, (h + 1) * P)
+                nc.tensor.matmul_mx(
+                    out=acc[:, h, :],
+                    lhsT=x_codes[i][:, tokens].bitcast(FP8X4),
+                    lhsT_scale=x_scales[i][:, tokens],
+                    rhs=w_codes[c][:].bitcast(FP8X4),
+                    rhs_scale=w_scales[c][:],
+                    start=True,
+                    stop=True,
+                )
+            res = keep.tile([P, TILES_PER_IMAGE, PART], F32, name="res%d%d" % (c, i))
+            nc.vector.tensor_tensor(out=res[:], in0=acc[:], in1=posb[:, :, cols], op=ADD)
+            nc.sync.dma_start(out=out[i].rearrange("(p h) n -> p h n", h=TILES_PER_IMAGE)[:, :, cols], in_=res[:])
+
+        nc.sync.dma_start(out=b_row[:], in_=b.unsqueeze(0))
+        nc.vector.memset(b_rows[:], 0.0)
+        nc.vector.memset(ones[:], 1.0)
+        make_identity(nc, ident[:])
+        load_x(0)
+        load_x(1)
         nc.sync.dma_start(out=pos_sb[:], in_=pos_emb.rearrange("(p h) n -> p h n", h=TILES_PER_IMAGE))
-        w_raw = keep.tile([P, PACK, F], BF16)
+        load_x(2)
+        load_x(3)
         nc.sync.dma_start(
             out=w_raw[:].rearrange("p (u e) n -> p u (e n)", u=2),
             in_=W.rearrange("(u p e) n -> p u (e n)", u=2, e=2),
         )
 
-        x_grp = []
-        for i in range(IMAGES):
-            xt = psum.tile([P, TILES_PER_IMAGE, 2, P], F32, name="xt%d" % i)
-            for half in range(2):
-                s = 2 * i + half
-                x_ord = keep.tile([P, 2, 256], BF16, name="x_ord%d" % s)
-                nc.vector.tensor_copy(
-                    out=x_ord[:].rearrange("p h (r c e) -> p h r c e", r=8, c=2),
-                    in_=x_raw[s][:].rearrange("p h (c r e) -> p h r c e", c=2, r=8),
-                )
-                for h in range(TILES_PER_IMAGE):
-                    nc.tensor.transpose(xt[:, h, half, :], x_ord[:, h, :].bitcast(F32), ident[:])
-            x_grp_i = keep.tile([P, TILES_PER_IMAGE * P * PACK], BF16, name="x_grp%d" % i, align_bytes=64)
-            nc.scalar.copy(
-                out=x_grp_i[:].bitcast(F32).rearrange("p (a x r) -> p a x r", x=8, r=2),
-                in_=xt[:].rearrange("p h s c -> p (h s c)").rearrange("p (a r x) -> p a x r", r=2, x=8),
-            )
-            x_grp.append(x_grp_i)
-
-        bias_ps = psum.tile([P, F], F32)
+        nc.vector.tensor_copy(out=b_rows[0:1, :], in_=b_row[:])
         nc.tensor.matmul(out=bias_ps[:], lhsT=ones[:], rhs=b_rows[:], start=True, stop=True)
-
-        x_codes = []
-        x_scales = []
         for i in range(IMAGES):
-            codes = keep.tile([P, TILES_PER_IMAGE * P], U32, name="x_codes%d" % i, align_bytes=64)
-            scales = keep.tile([P, TILES_PER_IMAGE * P], U8, name="x_scales%d" % i, align_bytes=64)
-            nc.vector.quantize_mx(out=codes[:].bitcast(FP8X4), scales=scales[:], in_=x_grp[i][:])
-            x_codes.append(codes)
-            x_scales.append(scales)
-        posb = keep.tile([P, TILES_PER_IMAGE, F], F32)
-        for h in range(TILES_PER_IMAGE):
-            nc.vector.tensor_tensor(out=posb[:, h, :], in0=bias_ps[:], in1=pos_sb[:, h, :], op=ADD)
-
-        w_codes = []
-        w_scales = []
+            transpose_x(2 * i)
+            transpose_x(2 * i + 1)
+            group_x(i)
+            add_b_to_pos(i)
         for c in range(W_PARTS):
-            w_grp = keep.tile([P, PART, PACK], BF16, name="w_grp%d" % c, align_bytes=64)
-            for copy, lo, hi in ((nc.vector.tensor_copy, 0, VECTOR_COLS), (nc.scalar.copy, VECTOR_COLS, PART)):
-                copy(
-                    out=w_grp[:, lo:hi, :].rearrange("p (a i) t -> p a t i", i=4),
-                    in_=w_raw[:, :, c * PART + lo : c * PART + hi].rearrange("p t (a i) -> p a t i", i=4),
-                )
-            codes = keep.tile([P, PART], U32, name="w_codes%d" % c, align_bytes=64)
-            scales = keep.tile([P, PART], U8, name="w_scales%d" % c, align_bytes=64)
-            nc.vector.quantize_mx(
-                out=codes[:].bitcast(FP8X4), scales=scales[:], in_=w_grp[:].rearrange("p n t -> p (n t)")
-            )
-            w_codes.append(codes)
-            w_scales.append(scales)
+            quantise_x(c)
+            regroup_w(c)
+            quantise_w(c)
 
         for c in range(W_PARTS):
-            cols = slice(c * PART, (c + 1) * PART)
             for i in range(IMAGES):
-                acc = psum.tile([P, TILES_PER_IMAGE, PART], F32, name="acc%d%d" % (c, i))
-                for h in range(TILES_PER_IMAGE):
-                    tokens = slice(h * P, (h + 1) * P)
-                    nc.tensor.matmul_mx(
-                        out=acc[:, h, :],
-                        lhsT=x_codes[i][:, tokens].bitcast(FP8X4),
-                        lhsT_scale=x_scales[i][:, tokens],
-                        rhs=w_codes[c][:].bitcast(FP8X4),
-                        rhs_scale=w_scales[c][:],
-                        start=True,
-                        stop=True,
-                    )
-                res = keep.tile([P, TILES_PER_IMAGE, PART], F32, name="res%d%d" % (c, i))
-                nc.vector.tensor_tensor(out=res[:], in0=acc[:], in1=posb[:, :, cols], op=ADD)
-                nc.sync.dma_start(
-                    out=out[i].rearrange("(p h) n -> p h n", h=TILES_PER_IMAGE)[:, :, cols], in_=res[:]
-                )
+                project(c, i)

@@ -21,7 +21,7 @@ TILES_PER_IMAGE = TOKEN_TILES // IMAGES
 
 W_PARTS = 2
 PART = F // W_PARTS
-VECTOR_COLS = 168
+VECTOR_COLS = 344
 FLOPS = 2 * TOKENS * K * F
 
 
@@ -77,12 +77,18 @@ def tile_resampling_s_kernel(tc, encoded, W, b, pos_emb, out):
         def add_b_to_pos(h):
             nc.vector.tensor_tensor(out=posb[:, h, :], in0=bias_ps[:], in1=pos_sb[:, h, :], op=ADD)
 
+        def regroup_columns(copy, c, lo, hi):
+            copy(
+                out=w_grp[c][:, lo - c * PART : hi - c * PART, :].rearrange("p (a i) t -> p a t i", i=4),
+                in_=w_raw[:, :, lo:hi].rearrange("p t (a i) -> p a t i", i=4),
+            )
+
         def regroup_w(c):
-            for copy, lo, hi in ((nc.vector.tensor_copy, 0, VECTOR_COLS), (nc.scalar.copy, VECTOR_COLS, PART)):
-                copy(
-                    out=w_grp[c][:, lo:hi, :].rearrange("p (a i) t -> p a t i", i=4),
-                    in_=w_raw[:, :, c * PART + lo : c * PART + hi].rearrange("p t (a i) -> p a t i", i=4),
-                )
+            split = min(max(VECTOR_COLS, c * PART), (c + 1) * PART)
+            if split > c * PART:
+                regroup_columns(nc.vector.tensor_copy, c, c * PART, split)
+            if split < (c + 1) * PART:
+                regroup_columns(nc.scalar.copy, c, split, (c + 1) * PART)
 
         def quantise_w(c):
             nc.vector.quantize_mx(

@@ -121,9 +121,9 @@ def tile_resampling_s_kernel(tc, encoded, W, b, pos_emb, out):
         make_identity(nc, ident[:])
         load_x(0)
         load_x(1)
-        nc.sync.dma_start(out=pos_sb[:], in_=pos_emb.rearrange("(p h) n -> p h n", h=TILES_PER_IMAGE))
         load_x(2)
         load_x(3)
+        nc.sync.dma_start(out=pos_sb[:], in_=pos_emb.rearrange("(p h) n -> p h n", h=TILES_PER_IMAGE))
         nc.sync.dma_start(
             out=w_raw[:].rearrange("p (u e) n -> p u (e n)", u=2),
             in_=W.rearrange("(u p e) n -> p u (e n)", u=2, e=2),
@@ -135,11 +135,14 @@ def tile_resampling_s_kernel(tc, encoded, W, b, pos_emb, out):
             transpose_x(2 * i)
             transpose_x(2 * i + 1)
             group_x(i)
-            add_b_to_pos(i)
+        for h in range(TILES_PER_IMAGE):
+            add_b_to_pos(h)
+        quantise_x(0)
         for c in range(W_PARTS):
-            quantise_x(c)
             regroup_w(c)
-            quantise_w(c)
+        quantise_w(0)
+        quantise_x(1)
+        quantise_w(1)
 
         for c in range(W_PARTS):
             for i in range(IMAGES):

@@ -121,9 +121,9 @@ def tile_resampling_s_kernel(tc, encoded, W, b, pos_emb, out):
         make_identity(nc, ident[:])
         load_x(0)
         load_x(1)
+        nc.sync.dma_start(out=pos_sb[:], in_=pos_emb.rearrange("(p h) n -> p h n", h=TILES_PER_IMAGE))
         load_x(2)
         load_x(3)
-        nc.sync.dma_start(out=pos_sb[:], in_=pos_emb.rearrange("(p h) n -> p h n", h=TILES_PER_IMAGE))
         nc.sync.dma_start(
             out=w_raw[:].rearrange("p (u e) n -> p u (e n)", u=2),
             in_=W.rearrange("(u p e) n -> p u (e n)", u=2, e=2),
@@ -135,8 +135,7 @@ def tile_resampling_s_kernel(tc, encoded, W, b, pos_emb, out):
             transpose_x(2 * i)
             transpose_x(2 * i + 1)
             group_x(i)
-        for h in range(TILES_PER_IMAGE):
-            add_b_to_pos(h)
+            add_b_to_pos(i)
         quantise_x(0)
         for c in range(W_PARTS):
             regroup_w(c)

from contextlib import ExitStack

import concourse.mybir as mybir
from concourse.masks import make_identity

BF16 = mybir.dt.bfloat16
F32 = mybir.dt.float32
U32 = mybir.dt.uint32
U8 = mybir.dt.uint8
FP8X4 = mybir.dt.float8_e4m3fn_x4
ADD = mybir.AluOpType.add

P = 128
PACK = 4
IMAGES = 2
TOKENS = 512
K = 512
F = 512
TOKEN_TILES = TOKENS // P
TILES_PER_IMAGE = TOKEN_TILES // IMAGES

W_PARTS = 2
PART = F // W_PARTS
VECTOR_COLS = 344
FLOPS = 2 * TOKENS * K * F


def tile_resampling_s_kernel(tc, encoded, W, b, pos_emb, out):
    nc = tc.nc
    with ExitStack() as ctx:
        keep = ctx.enter_context(tc.tile_pool(name="keep", bufs=1))
        psum = ctx.enter_context(tc.psum_pool(name="psum", bufs=1))
        ctx.enter_context(tc.manual_schedule())

        ident = keep.tile([P, P], F32)
        ones = keep.tile([P, P], BF16)
        b_row = keep.tile([1, F], BF16)
        b_rows = keep.tile([P, F], BF16)
        x_raw = [keep.tile([P, 2, 256], BF16, name="x_raw%d" % s) for s in range(TOKEN_TILES)]
        x_ord = [keep.tile([P, 2, 256], BF16, name="x_ord%d" % s) for s in range(TOKEN_TILES)]
        xt = [psum.tile([P, TILES_PER_IMAGE, 2, P], F32, name="xt%d" % i) for i in range(IMAGES)]
        x_cols = TILES_PER_IMAGE * P
        x_grp = [keep.tile([P, x_cols * PACK], BF16, name="x_grp%d" % i, align_bytes=64) for i in range(IMAGES)]
        x_codes = [keep.tile([P, x_cols], U32, name="x_codes%d" % i, align_bytes=64) for i in range(IMAGES)]
        x_scales = [keep.tile([P, x_cols], U8, name="x_scales%d" % i, align_bytes=64) for i in range(IMAGES)]
        pos_sb = keep.tile([P, TILES_PER_IMAGE, F], BF16)
        bias_ps = psum.tile([P, F], F32)
        posb = keep.tile([P, TILES_PER_IMAGE, F], F32)
        w_raw = keep.tile([P, PACK, F], BF16)
        w_grp = [keep.tile([P, PART, PACK], BF16, name="w_grp%d" % c, align_bytes=64) for c in range(W_PARTS)]
        w_codes = [keep.tile([P, PART], U32, name="w_codes%d" % c, align_bytes=64) for c in range(W_PARTS)]
        w_scales = [keep.tile([P, PART], U8, name="w_scales%d" % c, align_bytes=64) for c in range(W_PARTS)]

        pair_rows = encoded.rearrange("i (q c) d -> (i q) (c d)", c=2)
        pair_rows = pair_rows.rearrange("(s p h) w -> s p h w", p=P, h=2)

        def load_x(s):
            nc.sync.dma_start(out=x_raw[s][:], in_=pair_rows[s])

        def transpose_x(s):
            nc.vector.tensor_copy(
                out=x_ord[s][:].rearrange("p h (r c e) -> p h r c e", r=8, c=2),
                in_=x_raw[s][:].rearrange("p h (c r e) -> p h r c e", c=2, r=8),
            )
            for h in range(TILES_PER_IMAGE):
                nc.tensor.transpose(xt[s // 2][:, h, s % 2, :], x_ord[s][:, h, :].bitcast(F32), ident[:])

        def group_x(i):
            nc.scalar.copy(
                out=x_grp[i][:].bitcast(F32).rearrange("p (a x r) -> p a x r", x=8, r=2),
                in_=xt[i][:].rearrange("p h s c -> p (h s c)").rearrange("p (a r x) -> p a x r", r=2, x=8),
            )

        def quantise_x(i):
            nc.vector.quantize_mx(out=x_codes[i][:].bitcast(FP8X4), scales=x_scales[i][:], in_=x_grp[i][:])

        def add_b_to_pos(h):
            nc.vector.tensor_tensor(out=posb[:, h, :], in0=bias_ps[:], in1=pos_sb[:, h, :], op=ADD)

        def regroup_columns(copy, c, lo, hi):
            copy(
                out=w_grp[c][:, lo - c * PART : hi - c * PART, :].rearrange("p (a i) t -> p a t i", i=4),
                in_=w_raw[:, :, lo:hi].rearrange("p t (a i) -> p a t i", i=4),
            )

        def regroup_w(c):
            split = min(max(VECTOR_COLS, c * PART), (c + 1) * PART)
            if split > c * PART:
                regroup_columns(nc.vector.tensor_copy, c, c * PART, split)
            if split < (c + 1) * PART:
                regroup_columns(nc.scalar.copy, c, split, (c + 1) * PART)

        def quantise_w(c):
            nc.vector.quantize_mx(
                out=w_codes[c][:].bitcast(FP8X4),
                scales=w_scales[c][:],
                in_=w_grp[c][:].rearrange("p n t -> p (n t)"),
            )

        def project(c, i):
            cols = slice(c * PART, (c + 1) * PART)
            acc = psum.tile([P, TILES_PER_IMAGE, PART], F32, name="acc%d%d" % (c, i))
            for h in range(TILES_PER_IMAGE):
                tokens = slice(h * P, (h + 1) * P)
                nc.tensor.matmul_mx(
                    out=acc[:, h, :],
                    lhsT=x_codes[i][:, tokens].bitcast(FP8X4),
                    lhsT_scale=x_scales[i][:, tokens],
                    rhs=w_codes[c][:].bitcast(FP8X4),
                    rhs_scale=w_scales[c][:],
                    start=True,
                    stop=True,
                )
            res = keep.tile([P, TILES_PER_IMAGE, PART], F32, name="res%d%d" % (c, i))
            nc.vector.tensor_tensor(out=res[:], in0=acc[:], in1=posb[:, :, cols], op=ADD)
            nc.sync.dma_start(out=out[i].rearrange("(p h) n -> p h n", h=TILES_PER_IMAGE)[:, :, cols], in_=res[:])

        nc.sync.dma_start(out=b_row[:], in_=b.unsqueeze(0))
        nc.vector.memset(b_rows[:], 0.0)
        nc.vector.memset(ones[:], 1.0)
        make_identity(nc, ident[:])
        load_x(0)
        load_x(1)
        nc.sync.dma_start(out=pos_sb[:], in_=pos_emb.rearrange("(p h) n -> p h n", h=TILES_PER_IMAGE))
        load_x(2)
        load_x(3)
        nc.sync.dma_start(
            out=w_raw[:].rearrange("p (u e) n -> p u (e n)", u=2),
            in_=W.rearrange("(u p e) n -> p u (e n)", u=2, e=2),
        )

        nc.vector.tensor_copy(out=b_rows[0:1, :], in_=b_row[:])
        nc.tensor.matmul(out=bias_ps[:], lhsT=ones[:], rhs=b_rows[:], start=True, stop=True)
        for i in range(IMAGES):
            transpose_x(2 * i)
            transpose_x(2 * i + 1)
            group_x(i)
            add_b_to_pos(i)
        quantise_x(0)
        for c in range(W_PARTS):
            regroup_w(c)
        quantise_w(0)
        quantise_x(1)
        quantise_w(1)

        for c in range(W_PARTS):
            for i in range(IMAGES):
                project(c, i)
